import numpy as np
import ml_dtypes


def mxq(x, axis, fmt="e4m3"):
    dtype, down = {"e4m3": (ml_dtypes.float8_e4m3fn, 7), "e5m2": (ml_dtypes.float8_e5m2, 14)}[fmt]
    v = np.moveaxis(np.asarray(x, np.float32).astype(ml_dtypes.bfloat16).astype(np.float64), axis, -1)
    blocks = v.reshape(v.shape[:-1] + (-1, 32))
    amax = np.abs(blocks).max(-1, keepdims=True)
    byte = np.maximum(np.where(amax > 0, np.frexp(amax)[1] - 1 + 127, 0) - down, 1)
    scale = np.exp2(byte - 127.0)
    codes = (blocks / scale).astype(np.float32).astype(dtype).astype(np.float64)
    return np.moveaxis((codes * scale).reshape(v.shape), -1, axis)


WIDE = False


def mx_kscale(k):
    if not WIDE:
        return np.ones(k)
    levels = np.array([10, -10, 5, -5, 0])
    if k % 512:
        return np.exp2(np.random.permutation(np.resize(levels, k // 32))).repeat(32)
    a = np.empty((k // 512, 16))
    for p in range(k // 512):
        a[p, :8] = np.random.permutation(np.resize(levels, 8))
        for g in range(8):
            far = levels[np.abs(levels - a[p, g]) >= 10]
            a[p, g + 8] = far[np.random.randint(len(far))]
    return np.exp2(a.ravel()).repeat(32)


BF16 = ml_dtypes.bfloat16


def bf(x):
    return np.asarray(x, np.float32).astype(BF16)


def f64(x):
    return np.asarray(x).astype(np.float64)


B, N, H, D, C, O = 2048, 3, 1024, 256, 512, 256
F = D + D + C


def setup_inputs():
    s = mx_kscale(F)
    t = mx_kscale(H)
    ri, rt = mx_kscale(H), mx_kscale(H)
    return {
        "input_text": bf(np.random.standard_normal((B, D)) * s[:D])[:, None, :],
        "input_img": bf(np.random.standard_normal((B, D)) * s[D:D + D])[:, None, :],
        "input_compress": bf(np.random.standard_normal((B, C)) * s[D + D:]),
        "base_text_features": bf(np.random.standard_normal((B, N, H)) * rt),
        "base_img_features": bf(np.random.standard_normal((B, N, H)) * ri),
        "W_user": bf(np.random.standard_normal((H, F)) / np.sqrt(F) / s * t[:, None]),
        "b_user": bf(np.random.standard_normal(H) * 0.3 * t),
        "Wl_img": bf(np.random.standard_normal((O, H)) * 0.5 * np.sqrt(N / H) / ri),
        "bl_img": bf(np.random.standard_normal(O) * 0.2),
        "Wr_img": bf(np.random.standard_normal((O, H)) * 0.5 / np.sqrt(H) / t),
        "Wl_txt": bf(np.random.standard_normal((O, H)) * 0.5 * np.sqrt(N / H) / rt),
        "bl_txt": bf(np.random.standard_normal(O) * 0.2),
        "Wr_txt": bf(np.random.standard_normal((O, H)) * 0.5 / np.sqrt(H) / t),
    }


def reference(input_text, input_img, input_compress, base_text_features, base_img_features,
              W_user, b_user, Wl_img, bl_img, Wr_img, Wl_txt, bl_txt, Wr_txt):
    feat = np.concatenate([f64(input_text)[:, 0], f64(input_img)[:, 0], f64(input_compress)], axis=-1)
    u = (mxq(feat, 1, "e4m3") @ mxq(f64(W_user), 1, "e4m3").T) + f64(b_user)
    mean_img = f64(base_img_features).mean(axis=1)
    mean_txt = f64(base_text_features).mean(axis=1)
    uq = mxq(u, 1, "e4m3")
    out = ((mxq(mean_img, 1, "e4m3") @ mxq(f64(Wl_img), 1, "e4m3").T) + f64(bl_img)
           + (uq @ mxq(f64(Wr_img), 1, "e4m3").T)
           + (mxq(mean_txt, 1, "e4m3") @ mxq(f64(Wl_txt), 1, "e4m3").T) + f64(bl_txt)
           + (uq @ mxq(f64(Wr_txt), 1, "e4m3").T))
    return np.maximum(out, 0.0)

@@ -1,0 +1,415 @@
+from contextlib import ExitStack
+
+import concourse.mybir as mybir
+from concourse.masks import make_identity
+
+F32 = mybir.dt.float32
+BF16 = mybir.dt.bfloat16
+U32 = mybir.dt.uint32
+U8 = mybir.dt.uint8
+FP8X4 = mybir.dt.float8_e4m3fn_x4
+ACT = mybir.ActivationFunctionType
+ALU = mybir.AluOpType
+
+P = 128
+USERS, NODES, H, O = 2048, 3, 1024, 256
+ROUND = 2 * P
+PASSES = H // (4 * P)
+ORDER = (0, 1, 6, 2, 3, 7, 4, 5)
+VECTOR_ROUNDS = (6, 7)
+GROUP = P // NODES
+BLOCK = 3 * GROUP
+PE_USERS = ROUND * (len(ORDER) - len(VECTOR_ROUNDS))
+PE_BLOCKS = {0: ((0, 1), (2,)), 1: ((3,), (4,)), 2: ((5,), (6,)), 3: ((7,), (8,)), 4: ((9,), (10,)), 5: ((11,), (12,))}
+AHEAD = 3
+FLOPS = 2 * USERS * H * H + 4 * 2 * USERS * H * O
+
+
+def tile_graphlearner_ib_pa_t_kernel(
+    tc,
+    input_text,
+    input_img,
+    input_compress,
+    base_text_features,
+    base_img_features,
+    W_user,
+    b_user,
+    Wl_img,
+    bl_img,
+    Wr_img,
+    Wl_txt,
+    bl_txt,
+    Wr_txt,
+    out,
+):
+    nc = tc.nc
+    text_v = input_text.rearrange("(r p i) o d -> r p i (o d)", p=P, i=2)
+    imgf_v = input_img.rearrange("(r p i) o d -> r p i (o d)", p=P, i=2)
+    comp_v = input_compress.rearrange("(r p i) d -> r p i d", p=P, i=2)
+    bases = (base_img_features, base_text_features)
+    rows_v = tuple(b.rearrange("b n h -> (b n) h") for b in bases)
+    users_v = tuple(b.rearrange("(s p) n h -> s p n h", p=P) for b in bases)
+    out_v = out.rearrange("(s p) o -> s p o", p=P)
+    wu_v = W_user.rearrange("(g p t) f -> g p t f", p=P, t=4)
+
+    with ExitStack() as stack:
+        keep = stack.enter_context(tc.tile_pool(name="keep", bufs=1))
+        rows_pool = stack.enter_context(tc.tile_pool(name="rows", bufs=24))
+        work = stack.enter_context(tc.tile_pool(name="work", bufs=2))
+        deep = stack.enter_context(tc.tile_pool(name="deep", bufs=4))
+        psum = stack.enter_context(tc.psum_pool(name="psum", bufs=8))
+        stack.enter_context(tc.manual_schedule())
+
+        ident = keep.tile([P, P], F32, name="ident")
+        make_identity(nc, ident[:])
+        brow = keep.tile([P, 768], BF16, name="brow")
+        nc.gpsimd.memset(brow[:], 0.0)
+        nc.scalar.dma_start(out=brow[0:2, 0:512], in_=b_user.rearrange("(g f) -> g f", g=2))
+        nc.scalar.dma_start(out=brow[0:1, 512:768], in_=bl_img.rearrange("(a o) -> a o", a=1))
+        nc.scalar.dma_start(out=brow[1:2, 512:768], in_=bl_txt.rearrange("(a o) -> a o", a=1))
+        pick = keep.tile([P, GROUP], BF16, name="pick")
+        nc.gpsimd.memset(pick[:], 1.0)
+        nc.gpsimd.affine_select(
+            out=pick[:], in_=pick[:], pattern=[[-NODES, GROUP]], compare_op=ALU.is_ge, fill=0.0, base=0, channel_multiplier=1
+        )
+        nc.gpsimd.affine_select(
+            out=pick[:], in_=pick[:], pattern=[[NODES, GROUP]], compare_op=ALU.is_ge, fill=0.0, base=NODES - 1, channel_multiplier=-1
+        )
+        ident_bf = keep.tile([P, P], BF16, name="ident_bf")
+        make_identity(nc, ident_bf[:])
+        ones = keep.tile([P, P], BF16, name="ones")
+        nc.gpsimd.memset(ones[:], 1.0)
+        bu = keep.tile([P, PASSES, 4], F32, name="bu")
+        bu_wide = keep.tile([P, PASSES, P, 4], F32, name="bu_wide")
+        bl = keep.tile([P, O], F32, name="bl")
+
+        wu_codes = keep.tile([P, 8, PASSES, P], U32, name="wu_codes", align_bytes=64)
+        wu_scales = keep.tile([P, 8, PASSES, P], U8, name="wu_scales", align_bytes=64)
+        ws_codes = keep.tile([P, 4, PASSES, O], U32, name="ws_codes", align_bytes=64)
+        ws_scales = keep.tile([P, 4, PASSES, O], U8, name="ws_scales", align_bytes=64)
+
+        raw, wgroup, rows, vnodes, vsum, feats = {}, {}, {}, {}, {}, {}
+        mg, m_q, fg, f_q, ug, u_q, u_bank, o_bank, res = {}, {}, {}, {}, {}, {}, {}, {}, {}
+
+        def quantise(values, codes, scales):
+            nc.vector.quantize_mx(out=codes.bitcast(FP8X4), scales=scales, in_=values)
+
+        def new_bank():
+            return psum.tile([P, 4, P], F32, name="bank", tag="bank")
+
+        def load_rows(b):
+            for x in range(2):
+                for q in range(3 * b, min(3 * b + 3, -(-PE_USERS // GROUP))):
+                    t = rows_pool.tile([P, H], BF16, name="rows", tag="rows")
+                    nc.sync.dma_start(out=t[:], in_=rows_v[x][3 * GROUP * q : 3 * GROUP * q + P, :])
+                    rows[(x, q)] = t
+
+        def load_vector(s, x):
+            t = work.tile([P, NODES, H], BF16, name="vnodes", tag="vnodes", bufs=3)
+            nc.sync.dma_start(out=t[:], in_=users_v[x][s])
+            vnodes[(s, x)] = t
+
+        def load_feat(r):
+            t = work.tile([P, 2, H], BF16, name="feat", tag="feat")
+            nc.sync.dma_start(out=t[:, :, 0:256], in_=text_v[r])
+            nc.sync.dma_start(out=t[:, :, 256:512], in_=imgf_v[r])
+            nc.sync.dma_start(out=t[:, :, 512:1024], in_=comp_v[r])
+            feats[r] = t
+
+        def load_w_user(half):
+            t = work.tile([P, 4, H], BF16, name="w_raw", tag="w_raw")
+            for i in range(2):
+                nc.sync.dma_start(out=t[:, 2 * i : 2 * i + 2, :], in_=wu_v[half][:, 2 * i : 2 * i + 2, :])
+            raw[("u", half)] = t
+
+        def load_w_out(half):
+            t = work.tile([P, 4, H], BF16, name="w_raw", tag="w_raw")
+            for i, w in enumerate(((Wl_img, Wr_img), (Wl_txt, Wr_txt))[half]):
+                nc.sync.dma_start(out=t[:, 2 * i : 2 * i + 2, :], in_=w.rearrange("(p a) h -> p a h", a=2))
+            raw[("o", half)] = t
+
+        def transpose_words(bank, slot, words, g, h):
+            nc.tensor.transpose(out=bank[:, slot, :], in_=words[:, 256 * g + h : 256 * (g + 1) : 2], identity=ident[:])
+
+        def transpose_w_user(half):
+            wg = work.tile([P, 4, PASSES, 4 * P], BF16, name="wg", tag="wgroup", align_bytes=64)
+            wgroup[("u", half)] = wg
+            for t in range(4):
+                words = raw[("u", half)][:, t, :].bitcast(F32)
+                bank = new_bank()
+                for g in range(PASSES):
+                    for h in range(2):
+                        transpose_words(bank, 2 * g + h, words, g, h)
+                nc.scalar.copy(
+                    out=wg[:, t, :, :].bitcast(F32).rearrange("p g (r u) -> p g r u", u=2),
+                    in_=bank[:].rearrange("p (g u) r -> p g r u", u=2),
+                )
+
+        def quantise_w_user(half):
+            cs = slice(4 * half, 4 * half + 4)
+            quantise(
+                wgroup[("u", half)][:].rearrange("p j g w -> p (j g w)"),
+                wu_codes[:, cs].rearrange("p j g r -> p (j g r)"),
+                wu_scales[:, cs].rearrange("p j g r -> p (j g r)"),
+            )
+
+        def transpose_pairs(src, dst):
+            for g in range(PASSES):
+                bank = new_bank()
+                for i in range(2):
+                    for h in range(2):
+                        transpose_words(bank, 2 * i + h, src[:, i, :].bitcast(F32), g, h)
+                nc.scalar.copy(out=dst[:, g, :].bitcast(F32).rearrange("p (r k) -> p r k", k=4), in_=bank[:].rearrange("p k r -> p r k"))
+
+        def transpose_w_out(half):
+            wg = work.tile([P, 2, PASSES, 4 * O], BF16, name="wg", tag="wgroup", align_bytes=64)
+            wgroup[("o", half)] = wg
+            for i in range(2):
+                transpose_pairs(raw[("o", half)][:, 2 * i : 2 * i + 2, :], wg[:, i, :, :])
+
+        def quantise_w_out(half):
+            ms = slice(2 * half, 2 * half + 2)
+            quantise(
+                wgroup[("o", half)][:].rearrange("p m g w -> p (m g w)"),
+                ws_codes[:, ms].rearrange("p m g o -> p (m g o)"),
+                ws_scales[:, ms].rearrange("p m g o -> p (m g o)"),
+            )
+
+        def transpose_feat(r):
+            t = work.tile([P, PASSES, 4 * ROUND], BF16, name="fg", tag="fg", align_bytes=64)
+            fg[r] = t
+            transpose_pairs(feats[r], t)
+
+        def quantise_feat(r):
+            codes = work.tile([P, PASSES, ROUND], U32, name="f_codes", tag="f_codes", align_bytes=64)
+            scales = work.tile([P, PASSES, ROUND], U8, name="f_scales", tag="f_scales", align_bytes=64)
+            f_q[r] = (codes, scales)
+            quantise(
+                fg[r][:].rearrange("p g w -> p (g w)"),
+                codes[:].rearrange("p g n -> p (g n)"),
+                scales[:].rearrange("p g n -> p (g n)"),
+            )
+
+        def mean_tile(r):
+            if r not in mg:
+                t = deep.tile([P, 2, PASSES, ROUND, 4], BF16, name="mg", tag="mg", align_bytes=64)
+                mg[r] = t
+            return mg[r]
+
+        def mean_copy(x, g, first, count, bank):
+            lo = first
+            while lo < first + count:
+                r = lo // ROUND
+                hi = min(first + count, ROUND * (r + 1))
+                nc.scalar.activation(
+                    out=mean_tile(r)[:, x, g, lo - ROUND * r : hi - ROUND * r, :],
+                    in_=bank[:, :, lo - first : hi - first].rearrange("p t n -> p n t"),
+                    func=ACT.Copy,
+                    scale=1.0 / NODES,
+                )
+                lo = hi
+
+        def sum_block(b, x):
+            first = BLOCK * b
+            count = min(BLOCK, PE_USERS - first)
+            for g in range(PASSES):
+                bank = new_bank()
+                todo = [(j, t) for j in range(-(-count // GROUP)) for t in range(4)]
+                for j, t in todo:
+                    n = min(GROUP, count - GROUP * j)
+                    nc.tensor.matmul(
+                        out=bank[:, t, GROUP * j : GROUP * j + n],
+                        lhsT=rows[(x, 3 * b + j)][:, 512 * g + t : 512 * (g + 1) : 4],
+                        rhs=pick[:, 0:n],
+                        start=(j, t) == todo[0],
+                        stop=(j, t) == todo[-1],
+                    )
+                mean_copy(x, g, first, count, bank)
+
+        def vector_sum(s, x):
+            n = vnodes[(s, x)]
+            part = work.tile([P, 4, H // 4], F32, name="part", tag="part")
+            total = deep.tile([P, 4, H // 4], F32, name="total", tag="total")
+            vsum[(s, x)] = total
+            by_t = [n[:, i, :].rearrange("p (k t) -> p t k", t=4) for i in range(NODES)]
+            nc.vector.tensor_tensor(out=part[:], in0=by_t[0], in1=by_t[1], op=ALU.add)
+            nc.vector.tensor_tensor(out=total[:], in0=part[:], in1=by_t[2], op=ALU.add)
+
+        def transpose_sum(s, x):
+            for g in range(PASSES):
+                bank = new_bank()
+                for t in range(4):
+                    nc.tensor.transpose(out=bank[:, t, :], in_=vsum[(s, x)][:, t, P * g : P * (g + 1)], identity=ident[:])
+                mean_copy(x, g, P * s, P, bank)
+
+        def quantise_means(r):
+            codes = work.tile([P, 2, PASSES, ROUND], U32, name="m_codes", tag="m_codes", align_bytes=64)
+            scales = work.tile([P, 2, PASSES, ROUND], U8, name="m_scales", tag="m_scales", align_bytes=64)
+            m_q[r] = (codes, scales)
+            for x in range(2):
+                quantise(
+                    mg[r][:, x].rearrange("p g n t -> p (g n t)"),
+                    codes[:, x].rearrange("p g n -> p (g n)"),
+                    scales[:, x].rearrange("p g n -> p (g n)"),
+                )
+
+        def stage1(r, i):
+            codes, scales = f_q[r]
+            cols = slice(P * i, P * (i + 1))
+            u_bank[(r, i)] = []
+            for half in range(PASSES):
+                bank = new_bank()
+                u_bank[(r, i)].append(bank)
+                for t in range(4):
+                    for g in range(PASSES):
+                        nc.tensor.matmul_mx(
+                            out=bank[:, t, :],
+                            lhsT=wu_codes[:, 4 * half + t, g, :].bitcast(FP8X4),
+                            lhsT_scale=wu_scales[:, 4 * half + t, g, :],
+                            rhs=codes[:, g, cols].bitcast(FP8X4),
+                            rhs_scale=scales[:, g, cols],
+                            start=(g == 0),
+                            stop=(g == PASSES - 1),
+                        )
+
+        def copy_u(r, i):
+            t = work.tile([P, PASSES, P, 4], BF16, name="ug", tag="ug", align_bytes=64)
+            ug[(r, i)] = t
+            for half in range(PASSES):
+                nc.vector.tensor_tensor(
+                    out=t[:, half], in0=u_bank[(r, i)][half][:].rearrange("p t n -> p n t"), in1=bu_wide[:, half], op=ALU.add
+                )
+
+        def quantise_u(r, i):
+            codes = deep.tile([P, PASSES, P], U32, name="u_codes", tag="u_codes", align_bytes=64)
+            scales = deep.tile([P, PASSES, P], U8, name="u_scales", tag="u_scales", align_bytes=64)
+            u_q[(r, i)] = (codes, scales)
+            quantise(
+                ug[(r, i)][:].rearrange("p g n t -> p (g n t)"),
+                codes[:].rearrange("p g n -> p (g n)"),
+                scales[:].rearrange("p g n -> p (g n)"),
+            )
+
+        def stage2(r, i):
+            bank = psum.tile([P, O], F32, name="ob", tag="bank")
+            o_bank[(r, i)] = bank
+            m_codes, m_scales = m_q[r]
+            u_codes, u_scales = u_q[(r, i)]
+            cols = slice(P * i, P * (i + 1))
+            left = []
+            for g in range(PASSES):
+                left.append((u_codes[:, g, :], u_scales[:, g, :], 1, g))
+                left.append((u_codes[:, g, :], u_scales[:, g, :], 3, g))
+                left.append((m_codes[:, 0, g, cols], m_scales[:, 0, g, cols], 0, g))
+                left.append((m_codes[:, 1, g, cols], m_scales[:, 1, g, cols], 2, g))
+            for n, (codes, scales, m, g) in enumerate(left):
+                nc.tensor.matmul_mx(
+                    out=bank[:],
+                    lhsT=codes.bitcast(FP8X4),
+                    lhsT_scale=scales,
+                    rhs=ws_codes[:, m, g, :].bitcast(FP8X4),
+                    rhs_scale=ws_scales[:, m, g, :],
+                    start=(n == 0),
+                    stop=(n == len(left) - 1),
+                )
+
+        def add_bias(r, i):
+            t = deep.tile([P, O], F32, name="res", tag="res")
+            res[(r, i)] = t
+            nc.vector.tensor_tensor(out=t[:], in0=o_bank[(r, i)][:], in1=bl[:], op=ALU.add)
+
+        def relu(r, i):
+            nc.scalar.activation(out=res[(r, i)][:], in_=res[(r, i)][:], func=ACT.Relu)
+
+        def store(r, i):
+            nc.sync.dma_start(out=out_v[2 * r + i], in_=res[(r, i)][:])
+
+        HALVES = 2 * len(ORDER)
+
+        def half_at(s):
+            return (ORDER[s // 2], s % 2) if 0 <= s < HALVES else None
+
+        sum_at = {}
+        for k, r in enumerate(ORDER):
+            if r in VECTOR_ROUNDS:
+                for n in range(4):
+                    sum_at[2 * k - 3 + n] = (2 * r + n // 2, n % 2)
+
+        def load_means(s):
+            if half_at(s) is not None:
+                r, i = half_at(s)
+                if r in PE_BLOCKS:
+                    for b in PE_BLOCKS[r][i]:
+                        load_rows(b)
+
+        load_w_user(0)
+        load_w_user(1)
+        load_feat(ORDER[0])
+        load_means(0)
+        load_w_out(0)
+        load_means(1)
+        load_feat(ORDER[1])
+        load_w_out(1)
+        load_vector(*sum_at[1])
+        load_means(2)
+        load_vector(*sum_at[2])
+
+        transpose_w_user(0)
+        transpose_w_user(1)
+        quantise_w_user(0)
+        transpose_feat(ORDER[0])
+        quantise_w_user(1)
+        bank = psum.tile([P, 4, P], BF16, name="bank_bf", tag="bank")
+        for t in range(4):
+            nc.tensor.transpose(out=bank[:, t, :], in_=brow[:, t:512:4], identity=ident_bf[:])
+        nc.vector.tensor_copy(out=bu[:], in_=bank[:, :, 0:PASSES].rearrange("p t g -> p g t"))
+        bank = psum.tile([P, O], F32, name="bank_bl", tag="bank")
+        nc.tensor.matmul(out=bank[:], lhsT=ones[:], rhs=brow[:, 512:768], start=True, stop=True)
+        nc.scalar.copy(out=bl[:], in_=bank[:])
+        quantise_feat(ORDER[0])
+        for half in range(PASSES):
+            nc.vector.tensor_copy(out=bu_wide[:, half], in_=bu[:, half : half + 1, :].to_broadcast([P, P, 4]))
+
+        for s in range(HALVES + 4):
+            here = half_at(s)
+            if half_at(s - 5) is not None:
+                store(*half_at(s - 5))
+            if s > 0:
+                load_means(s + AHEAD - 1)
+                if s + 2 in sum_at:
+                    load_vector(*sum_at[s + 2])
+            if s % 2 == 0 and half_at(s + 4) is not None:
+                load_feat(half_at(s + 4)[0])
+            if half_at(s - 4) is not None:
+                add_bias(*half_at(s - 4))
+            if here is not None:
+                r, i = here
+                for x in range(2):
+                    if r in PE_BLOCKS:
+                        for b in PE_BLOCKS[r][i]:
+                            sum_block(b, x)
+                    else:
+                        transpose_sum(2 * r + i, x)
+            if s % 2 == 0 and half_at(s + 2) is not None:
+                transpose_feat(half_at(s + 2)[0])
+            if s in (0, 1):
+                transpose_w_out(s)
+            if half_at(s - 4) is not None:
+                relu(*half_at(s - 4))
+            if half_at(s - 3) is not None:
+                stage2(*half_at(s - 3))
+            if here is not None:
+                stage1(*here)
+            if s % 2 == 0 and half_at(s - 2) is not None:
+                quantise_means(half_at(s - 2)[0])
+            if s in (1, 2):
+                quantise_w_out(s - 1)
+            if half_at(s - 1) is not None:
+                quantise_u(*half_at(s - 1))
+            if s in sum_at:
+                vector_sum(*sum_at[s])
+            if s % 2 == 1 and half_at(s + 1) is not None:
+                quantise_feat(half_at(s + 1)[0])
+            if here is not None:
+                copy_u(*here)
+        store(*half_at(HALVES - 1))

@@ -62,11 +62,11 @@ def tile_graphlearner_ib_pa_t_kernel(
 
         ident = keep.tile([P, P], F32, name="ident")
         make_identity(nc, ident[:])
+        warm = keep.tile([P, 1], F32, name="warm")
+        nc.vector.memset(warm[:], 0.0)
+        nc.scalar.activation(out=warm[:], in_=warm[:], func=ACT.Relu)
         brow = keep.tile([P, 768], BF16, name="brow")
         nc.gpsimd.memset(brow[:], 0.0)
-        nc.scalar.dma_start(out=brow[0:2, 0:512], in_=b_user.rearrange("(g f) -> g f", g=2))
-        nc.scalar.dma_start(out=brow[0:1, 512:768], in_=bl_img.rearrange("(a o) -> a o", a=1))
-        nc.scalar.dma_start(out=brow[1:2, 512:768], in_=bl_txt.rearrange("(a o) -> a o", a=1))
         pick = keep.tile([P, GROUP], BF16, name="pick")
         nc.gpsimd.memset(pick[:], 1.0)
         nc.gpsimd.affine_select(
@@ -118,8 +118,8 @@ def tile_graphlearner_ib_pa_t_kernel(
 
         def load_w_user(half):
             t = work.tile([P, 4, H], BF16, name="w_raw", tag="w_raw")
-            for i in range(2):
-                nc.sync.dma_start(out=t[:, 2 * i : 2 * i + 2, :], in_=wu_v[half][:, 2 * i : 2 * i + 2, :])
+            for i in range(4):
+                nc.sync.dma_start(out=t[:, i : i + 1, :], in_=wu_v[half][:, i : i + 1, :])
             raw[("u", half)] = t
 
         def load_w_out(half):
@@ -322,7 +322,7 @@ def tile_graphlearner_ib_pa_t_kernel(
             nc.scalar.activation(out=res[(r, i)][:], in_=res[(r, i)][:], func=ACT.Relu)
 
         def store(r, i):
-            nc.sync.dma_start(out=out_v[2 * r + i], in_=res[(r, i)][:])
+            nc.scalar.dma_start(out=out_v[2 * r + i], in_=res[(r, i)][:])
 
         HALVES = 2 * len(ORDER)
 
@@ -344,11 +344,14 @@ def tile_graphlearner_ib_pa_t_kernel(
 
         load_w_user(0)
         load_w_user(1)
+        nc.sync.dma_start(out=brow[0:2, 0:512], in_=b_user.rearrange("(g f) -> g f", g=2))
+        nc.sync.dma_start(out=brow[0:1, 512:768], in_=bl_img.rearrange("(a o) -> a o", a=1))
+        nc.sync.dma_start(out=brow[1:2, 512:768], in_=bl_txt.rearrange("(a o) -> a o", a=1))
         load_feat(ORDER[0])
         load_means(0)
+        load_feat(ORDER[1])
         load_w_out(0)
         load_means(1)
-        load_feat(ORDER[1])
         load_w_out(1)
         load_vector(*sum_at[1])
         load_means(2)
@@ -370,10 +373,8 @@ def tile_graphlearner_ib_pa_t_kernel(
         for half in range(PASSES):
             nc.vector.tensor_copy(out=bu_wide[:, half], in_=bu[:, half : half + 1, :].to_broadcast([P, P, 4]))
 
-        for s in range(HALVES + 4):
+        for s in range(HALVES + 3):
             here = half_at(s)
-            if half_at(s - 5) is not None:
-                store(*half_at(s - 5))
             if s > 0:
                 load_means(s + AHEAD - 1)
                 if s + 2 in sum_at:
@@ -381,8 +382,11 @@ def tile_graphlearner_ib_pa_t_kernel(
             if s % 2 == 0 and half_at(s + 4) is not None:
                 load_feat(half_at(s + 4)[0])
             if half_at(s - 4) is not None:
-                add_bias(*half_at(s - 4))
+                store(*half_at(s - 4))
+            if half_at(s - 3) is not None:
+                stage2(*half_at(s - 3))
             if here is not None:
+                stage1(*here)
                 r, i = here
                 for x in range(2):
                     if r in PE_BLOCKS:
@@ -394,22 +398,20 @@ def tile_graphlearner_ib_pa_t_kernel(
                 transpose_feat(half_at(s + 2)[0])
             if s in (0, 1):
                 transpose_w_out(s)
-            if half_at(s - 4) is not None:
-                relu(*half_at(s - 4))
-            if half_at(s - 3) is not None:
-                stage2(*half_at(s - 3))
-            if here is not None:
-                stage1(*here)
             if s % 2 == 0 and half_at(s - 2) is not None:
                 quantise_means(half_at(s - 2)[0])
             if s in (1, 2):
                 quantise_w_out(s - 1)
             if half_at(s - 1) is not None:
                 quantise_u(*half_at(s - 1))
-            if s in sum_at:
-                vector_sum(*sum_at[s])
             if s % 2 == 1 and half_at(s + 1) is not None:
                 quantise_feat(half_at(s + 1)[0])
+            if half_at(s - 3) is not None:
+                add_bias(*half_at(s - 3))
             if here is not None:
                 copy_u(*here)
+            if s in sum_at:
+                vector_sum(*sum_at[s])
+            if half_at(s - 3) is not None:
+                relu(*half_at(s - 3))
         store(*half_at(HALVES - 1))

@@ -21,7 +21,7 @@ GROUP = P // NODES
 BLOCK = 3 * GROUP
 PE_USERS = ROUND * (len(ORDER) - len(VECTOR_ROUNDS))
 PE_BLOCKS = {0: ((0, 1), (2,)), 1: ((3,), (4,)), 2: ((5,), (6,)), 3: ((7,), (8,)), 4: ((9,), (10,)), 5: ((11,), (12,))}
-AHEAD = 3
+LEAD = 2
 FLOPS = 2 * USERS * H * H + 4 * 2 * USERS * H * O
 
 
@@ -88,7 +88,7 @@ def tile_graphlearner_ib_pa_t_kernel(
         ws_codes = keep.tile([P, 4, PASSES, O], U32, name="ws_codes", align_bytes=64)
         ws_scales = keep.tile([P, 4, PASSES, O], U8, name="ws_scales", align_bytes=64)
 
-        raw, wgroup, rows, vnodes, vsum, feats = {}, {}, {}, {}, {}, {}
+        raw, wgroup, rows, vnodes, vsum, vmean, feats = {}, {}, {}, {}, {}, {}, {}
         mg, m_q, fg, f_q, ug, u_q, u_bank, o_bank, res = {}, {}, {}, {}, {}, {}, {}, {}, {}
 
         def quantise(values, codes, scales):
@@ -110,7 +110,7 @@ def tile_graphlearner_ib_pa_t_kernel(
             vnodes[(s, x)] = t
 
         def load_feat(r):
-            t = work.tile([P, 2, H], BF16, name="feat", tag="feat")
+            t = work.tile([P, 2, H], BF16, name="feat", tag="feat", bufs=3)
             nc.sync.dma_start(out=t[:, :, 0:256], in_=text_v[r])
             nc.sync.dma_start(out=t[:, :, 256:512], in_=imgf_v[r])
             nc.sync.dma_start(out=t[:, :, 512:1024], in_=comp_v[r])
@@ -209,38 +209,47 @@ def tile_graphlearner_ib_pa_t_kernel(
                 )
                 lo = hi
 
-        def sum_block(b, x):
+        def sum_block(b, x, g):
             first = BLOCK * b
             count = min(BLOCK, PE_USERS - first)
-            for g in range(PASSES):
-                bank = new_bank()
-                todo = [(j, t) for j in range(-(-count // GROUP)) for t in range(4)]
-                for j, t in todo:
-                    n = min(GROUP, count - GROUP * j)
-                    nc.tensor.matmul(
-                        out=bank[:, t, GROUP * j : GROUP * j + n],
-                        lhsT=rows[(x, 3 * b + j)][:, 512 * g + t : 512 * (g + 1) : 4],
-                        rhs=pick[:, 0:n],
-                        start=(j, t) == todo[0],
-                        stop=(j, t) == todo[-1],
-                    )
-                mean_copy(x, g, first, count, bank)
+            bank = new_bank()
+            todo = [(j, t) for j in range(-(-count // GROUP)) for t in range(4)]
+            for j, t in todo:
+                n = min(GROUP, count - GROUP * j)
+                nc.tensor.matmul(
+                    out=bank[:, t, GROUP * j : GROUP * j + n],
+                    lhsT=rows[(x, 3 * b + j)][:, 512 * g + t : 512 * (g + 1) : 4],
+                    rhs=pick[:, 0:n],
+                    start=(j, t) == todo[0],
+                    stop=(j, t) == todo[-1],
+                )
+            mean_copy(x, g, first, count, bank)
 
         def vector_sum(s, x):
             n = vnodes[(s, x)]
-            part = work.tile([P, 4, H // 4], F32, name="part", tag="part")
-            total = deep.tile([P, 4, H // 4], F32, name="total", tag="total")
+            part = work.tile([P, 2, H // 4, 2], F32, name="part", tag="part")
+            total = work.tile([P, 2, H // 4, 2], F32, name="total", tag="total", bufs=3)
             vsum[(s, x)] = total
-            by_t = [n[:, i, :].rearrange("p (k t) -> p t k", t=4) for i in range(NODES)]
-            nc.vector.tensor_tensor(out=part[:], in0=by_t[0], in1=by_t[1], op=ALU.add)
-            nc.vector.tensor_tensor(out=total[:], in0=part[:], in1=by_t[2], op=ALU.add)
+            by_h = [n[:, i, :].rearrange("p (m h e) -> p h m e", h=2, e=2) for i in range(NODES)]
+            nc.vector.tensor_tensor(out=part[:], in0=by_h[0], in1=by_h[1], op=ALU.add)
+            nc.vector.tensor_tensor(out=total[:], in0=part[:], in1=by_h[2], op=ALU.add)
+
+        def scale_sum(s, x):
+            t = deep.tile([P, H], BF16, name="mean", tag="mean")
+            vmean[(s, x)] = t
+            nc.scalar.activation(out=t[:], in_=vsum[(s, x)][:].rearrange("p h m e -> p (h m e)"), func=ACT.Copy, scale=1.0 / NODES)
 
         def transpose_sum(s, x):
+            words = vmean[(s, x)][:].bitcast(F32)
+            bank = new_bank()
             for g in range(PASSES):
-                bank = new_bank()
-                for t in range(4):
-                    nc.tensor.transpose(out=bank[:, t, :], in_=vsum[(s, x)][:, t, P * g : P * (g + 1)], identity=ident[:])
-                mean_copy(x, g, P * s, P, bank)
+                for h in range(2):
+                    nc.tensor.transpose(out=bank[:, 2 * g + h, :], in_=words[:, 256 * h + P * g : 256 * h + P * (g + 1)], identity=ident[:])
+            r, i = divmod(s, 2)
+            nc.scalar.copy(
+                out=mean_tile(r)[:, x, :, P * i : P * (i + 1), :].rearrange("p g n t -> p g (n t)").bitcast(F32).rearrange("p g (n h) -> p g n h", h=2),
+                in_=bank[:].rearrange("p (g h) n -> p g n h", h=2),
+            )
 
         def quantise_means(r):
             codes = work.tile([P, 2, PASSES, ROUND], U32, name="m_codes", tag="m_codes", align_bytes=64)
@@ -253,36 +262,34 @@ def tile_graphlearner_ib_pa_t_kernel(
                     scales[:, x].rearrange("p g n -> p (g n)"),
                 )
 
-        def stage1(r, i):
+        def stage1(r, i, half):
             codes, scales = f_q[r]
             cols = slice(P * i, P * (i + 1))
-            u_bank[(r, i)] = []
-            for half in range(PASSES):
-                bank = new_bank()
-                u_bank[(r, i)].append(bank)
-                for t in range(4):
-                    for g in range(PASSES):
-                        nc.tensor.matmul_mx(
-                            out=bank[:, t, :],
-                            lhsT=wu_codes[:, 4 * half + t, g, :].bitcast(FP8X4),
-                            lhsT_scale=wu_scales[:, 4 * half + t, g, :],
-                            rhs=codes[:, g, cols].bitcast(FP8X4),
-                            rhs_scale=scales[:, g, cols],
-                            start=(g == 0),
-                            stop=(g == PASSES - 1),
-                        )
+            bank = new_bank()
+            u_bank[(r, i, half)] = bank
+            for t in range(4):
+                for g in range(PASSES):
+                    nc.tensor.matmul_mx(
+                        out=bank[:, t, :],
+                        lhsT=wu_codes[:, 4 * half + t, g, :].bitcast(FP8X4),
+                        lhsT_scale=wu_scales[:, 4 * half + t, g, :],
+                        rhs=codes[:, g, cols].bitcast(FP8X4),
+                        rhs_scale=scales[:, g, cols],
+                        start=(g == 0),
+                        stop=(g == PASSES - 1),
+                    )
 
         def copy_u(r, i):
-            t = work.tile([P, PASSES, P, 4], BF16, name="ug", tag="ug", align_bytes=64)
-            ug[(r, i)] = t
+            ut = work.tile([P, PASSES, P, 4], BF16, name="ug", tag="ug", align_bytes=64)
+            ug[(r, i)] = ut
             for half in range(PASSES):
                 nc.vector.tensor_tensor(
-                    out=t[:, half], in0=u_bank[(r, i)][half][:].rearrange("p t n -> p n t"), in1=bu_wide[:, half], op=ALU.add
+                    out=ut[:, half], in0=u_bank[(r, i, half)][:].rearrange("p t n -> p n t"), in1=bu_wide[:, half], op=ALU.add
                 )
 
         def quantise_u(r, i):
-            codes = deep.tile([P, PASSES, P], U32, name="u_codes", tag="u_codes", align_bytes=64)
-            scales = deep.tile([P, PASSES, P], U8, name="u_scales", tag="u_scales", align_bytes=64)
+            codes = deep.tile([P, PASSES, P], U32, name="u_codes", tag="u_codes", align_bytes=64, bufs=7)
+            scales = deep.tile([P, PASSES, P], U8, name="u_scales", tag="u_scales", align_bytes=64, bufs=7)
             u_q[(r, i)] = (codes, scales)
             quantise(
                 ug[(r, i)][:].rearrange("p g n t -> p (g n t)"),
@@ -329,34 +336,33 @@ def tile_graphlearner_ib_pa_t_kernel(
         def half_at(s):
             return (ORDER[s // 2], s % 2) if 0 <= s < HALVES else None
 
-        sum_at = {}
-        for k, r in enumerate(ORDER):
-            if r in VECTOR_ROUNDS:
-                for n in range(4):
-                    sum_at[2 * k - 3 + n] = (2 * r + n // 2, n % 2)
-
-        def load_means(s):
-            if half_at(s) is not None:
-                r, i = half_at(s)
-                if r in PE_BLOCKS:
-                    for b in PE_BLOCKS[r][i]:
-                        load_rows(b)
-
+        sum_at = {0: (12, 0), 1: (12, 1), 2: (13, 0), 3: (13, 1), 6: (14, 0), 7: (14, 1), 8: (15, 0), 9: (15, 1)}
+        loads = []
+        for s in range(HALVES):
+            r, i = half_at(s)
+            if r in PE_BLOCKS:
+                for b in PE_BLOCKS[r][i]:
+                    loads.append((s, 1, load_rows, (b,)))
+            if s in sum_at:
+                loads.append((s, 2, load_vector, sum_at[s]))
+            if i == 0:
+                loads.append((s - LEAD - 2, 0, load_feat, (r,)))
+        for half in range(2):
+            loads.append((half, 3, load_w_out, (half,)))
+        loads = sorted(loads, key=lambda l: l[0:2])
         load_w_user(0)
         load_w_user(1)
-        nc.sync.dma_start(out=brow[0:2, 0:512], in_=b_user.rearrange("(g f) -> g f", g=2))
-        nc.sync.dma_start(out=brow[0:1, 512:768], in_=bl_img.rearrange("(a o) -> a o", a=1))
-        nc.sync.dma_start(out=brow[1:2, 512:768], in_=bl_txt.rearrange("(a o) -> a o", a=1))
-        load_feat(ORDER[0])
-        load_means(0)
-        load_feat(ORDER[1])
-        load_w_out(0)
-        load_means(1)
-        load_w_out(1)
-        load_vector(*sum_at[1])
-        load_means(2)
-        load_vector(*sum_at[2])
+        nc.gpsimd.dma_start(out=brow[0:2, 0:512], in_=b_user.rearrange("(g f) -> g f", g=2))
+        nc.gpsimd.dma_start(out=brow[0:1, 512:768], in_=bl_img.rearrange("(a o) -> a o", a=1))
+        nc.gpsimd.dma_start(out=brow[1:2, 512:768], in_=bl_txt.rearrange("(a o) -> a o", a=1))
 
+        def load_until(limit):
+            for item in [l for l in loads if l[0] <= limit]:
+                loads.remove(item)
+                need, kind, call, args = item
+                call(*args)
+
+        load_until(2 - 1)
         transpose_w_user(0)
         transpose_w_user(1)
         quantise_w_user(0)
@@ -366,50 +372,54 @@ def tile_graphlearner_ib_pa_t_kernel(
         for t in range(4):
             nc.tensor.transpose(out=bank[:, t, :], in_=brow[:, t:512:4], identity=ident_bf[:])
         nc.vector.tensor_copy(out=bu[:], in_=bank[:, :, 0:PASSES].rearrange("p t g -> p g t"))
-        bank = psum.tile([P, O], F32, name="bank_bl", tag="bank")
-        nc.tensor.matmul(out=bank[:], lhsT=ones[:], rhs=brow[:, 512:768], start=True, stop=True)
-        nc.scalar.copy(out=bl[:], in_=bank[:])
         quantise_feat(ORDER[0])
         for half in range(PASSES):
             nc.vector.tensor_copy(out=bu_wide[:, half], in_=bu[:, half : half + 1, :].to_broadcast([P, P, 4]))
 
-        for s in range(HALVES + 3):
-            here = half_at(s)
-            if s > 0:
-                load_means(s + AHEAD - 1)
-                if s + 2 in sum_at:
-                    load_vector(*sum_at[s + 2])
-            if s % 2 == 0 and half_at(s + 4) is not None:
-                load_feat(half_at(s + 4)[0])
+        for s in range(-LEAD, HALVES + 3):
+            load_until(s + 2)
             if half_at(s - 4) is not None:
                 store(*half_at(s - 4))
-            if half_at(s - 3) is not None:
-                stage2(*half_at(s - 3))
-            if here is not None:
-                stage1(*here)
-                r, i = here
+            if s - 1 in sum_at:
+                scale_sum(*sum_at[s - 1])
+            todo = []
+            if half_at(s) is not None:
+                r, i = half_at(s)
                 for x in range(2):
                     if r in PE_BLOCKS:
                         for b in PE_BLOCKS[r][i]:
-                            sum_block(b, x)
+                            for g in range(PASSES):
+                                todo.append((sum_block, (b, x, g)))
                     else:
-                        transpose_sum(2 * r + i, x)
-            if s % 2 == 0 and half_at(s + 2) is not None:
-                transpose_feat(half_at(s + 2)[0])
+                        todo.append((transpose_sum, (2 * r + i, x)))
+            if half_at(s - 3) is not None:
+                stage2(*half_at(s - 3))
+            for half in range(PASSES):
+                if half_at(s + LEAD) is not None:
+                    r, i = half_at(s + LEAD)
+                    stage1(r, i, half)
+            for call, args in todo:
+                call(*args)
+            if (s + LEAD) % 2 == 0 and half_at(s + LEAD + 2) is not None:
+                transpose_feat(half_at(s + LEAD + 2)[0])
             if s in (0, 1):
                 transpose_w_out(s)
-            if s % 2 == 0 and half_at(s - 2) is not None:
-                quantise_means(half_at(s - 2)[0])
             if s in (1, 2):
                 quantise_w_out(s - 1)
-            if half_at(s - 1) is not None:
-                quantise_u(*half_at(s - 1))
-            if s % 2 == 1 and half_at(s + 1) is not None:
-                quantise_feat(half_at(s + 1)[0])
+            if s == 0:
+                bank = psum.tile([P, O], F32, name="bank_bl", tag="bank")
+                nc.tensor.matmul(out=bank[:], lhsT=ones[:], rhs=brow[:, 512:768], start=True, stop=True)
+                nc.scalar.copy(out=bl[:], in_=bank[:])
+            if s % 2 == 0 and half_at(s - 2) is not None:
+                quantise_means(half_at(s - 2)[0])
+            if half_at(s + LEAD - 1) is not None:
+                quantise_u(*half_at(s + LEAD - 1))
+            if (s + LEAD) % 2 == 1 and half_at(s + LEAD + 1) is not None:
+                quantise_feat(half_at(s + LEAD + 1)[0])
             if half_at(s - 3) is not None:
                 add_bias(*half_at(s - 3))
-            if here is not None:
-                copy_u(*here)
+            if half_at(s + LEAD) is not None:
+                copy_u(*half_at(s + LEAD))
             if s in sum_at:
                 vector_sum(*sum_at[s])
             if half_at(s - 3) is not None:

@@ -16,12 +16,13 @@ USERS, NODES, H, O = 2048, 3, 1024, 256
 ROUND = 2 * P
 PASSES = H // (4 * P)
 ORDER = (0, 1, 6, 2, 3, 7, 4, 5)
-VECTOR_ROUNDS = (6, 7)
+VECTOR_ROUNDS = (6, 7,)
 GROUP = P // NODES
 BLOCK = 3 * GROUP
 PE_USERS = ROUND * (len(ORDER) - len(VECTOR_ROUNDS))
 PE_BLOCKS = {0: ((0, 1), (2,)), 1: ((3,), (4,)), 2: ((5,), (6,)), 3: ((7,), (8,)), 4: ((9,), (10,)), 5: ((11,), (12,))}
-LEAD = 2
+LEAD = 4
+EARLY = {-3: (0,), -1: (1,)}
 FLOPS = 2 * USERS * H * H + 4 * 2 * USERS * H * O
 
 
@@ -54,7 +55,7 @@ def tile_graphlearner_ib_pa_t_kernel(
 
     with ExitStack() as stack:
         keep = stack.enter_context(tc.tile_pool(name="keep", bufs=1))
-        rows_pool = stack.enter_context(tc.tile_pool(name="rows", bufs=24))
+        rows_pool = stack.enter_context(tc.tile_pool(name="rows", bufs=18))
         work = stack.enter_context(tc.tile_pool(name="work", bufs=2))
         deep = stack.enter_context(tc.tile_pool(name="deep", bufs=4))
         psum = stack.enter_context(tc.psum_pool(name="psum", bufs=8))
@@ -140,7 +141,8 @@ def tile_graphlearner_ib_pa_t_kernel(
                 for g in range(PASSES):
                     for h in range(2):
                         transpose_words(bank, 2 * g + h, words, g, h)
-                nc.scalar.copy(
+                copy = nc.scalar.copy if t % 2 == 0 else nc.vector.tensor_copy
+                copy(
                     out=wg[:, t, :, :].bitcast(F32).rearrange("p g (r u) -> p g r u", u=2),
                     in_=bank[:].rearrange("p (g u) r -> p g r u", u=2),
                 )
@@ -192,7 +194,7 @@ def tile_graphlearner_ib_pa_t_kernel(
 
         def mean_tile(r):
             if r not in mg:
-                t = deep.tile([P, 2, PASSES, ROUND, 4], BF16, name="mg", tag="mg", align_bytes=64)
+                t = deep.tile([P, 2, PASSES, ROUND, 4], BF16, name="mg", tag="mg", align_bytes=64, bufs=3)
                 mg[r] = t
             return mg[r]
 
@@ -255,12 +257,22 @@ def tile_graphlearner_ib_pa_t_kernel(
             codes = work.tile([P, 2, PASSES, ROUND], U32, name="m_codes", tag="m_codes", align_bytes=64)
             scales = work.tile([P, 2, PASSES, ROUND], U8, name="m_scales", tag="m_scales", align_bytes=64)
             m_q[r] = (codes, scales)
+            quantise(
+                mg[r][:].rearrange("p x g n t -> p (x g n t)"),
+                codes[:].rearrange("p x g n -> p (x g n)"),
+                scales[:].rearrange("p x g n -> p (x g n)"),
+            )
+
+        def quantise_half(r, i):
+            if i == 0:
+                codes = work.tile([P, 2, PASSES, ROUND], U32, name="m_codes", tag="m_codes", align_bytes=64)
+                scales = work.tile([P, 2, PASSES, ROUND], U8, name="m_scales", tag="m_scales", align_bytes=64)
+                m_q[r] = (codes, scales)
+            codes, scales = m_q[r]
+            cols = slice(P * i, P * (i + 1))
             for x in range(2):
-                quantise(
-                    mg[r][:, x].rearrange("p g n t -> p (g n t)"),
-                    codes[:, x].rearrange("p g n -> p (g n)"),
-                    scales[:, x].rearrange("p g n -> p (g n)"),
-                )
+                for g in range(PASSES):
+                    quantise(mg[r][:, x, g, cols].rearrange("p n t -> p (n t)"), codes[:, x, g, cols], scales[:, x, g, cols])
 
         def stage1(r, i, half):
             codes, scales = f_q[r]
@@ -288,8 +300,8 @@ def tile_graphlearner_ib_pa_t_kernel(
                 )
 
         def quantise_u(r, i):
-            codes = deep.tile([P, PASSES, P], U32, name="u_codes", tag="u_codes", align_bytes=64, bufs=7)
-            scales = deep.tile([P, PASSES, P], U8, name="u_scales", tag="u_scales", align_bytes=64, bufs=7)
+            codes = deep.tile([P, PASSES, P], U32, name="u_codes", tag="u_codes", align_bytes=64, bufs=8)
+            scales = deep.tile([P, PASSES, P], U8, name="u_scales", tag="u_scales", align_bytes=64, bufs=8)
             u_q[(r, i)] = (codes, scales)
             quantise(
                 ug[(r, i)][:].rearrange("p g n t -> p (g n t)"),
@@ -342,7 +354,7 @@ def tile_graphlearner_ib_pa_t_kernel(
             r, i = half_at(s)
             if r in PE_BLOCKS:
                 for b in PE_BLOCKS[r][i]:
-                    loads.append((s, 1, load_rows, (b,)))
+                    loads.append((s if b > 0 else min(EARLY), 1, load_rows, (b,)))
             if s in sum_at:
                 loads.append((s, 2, load_vector, sum_at[s]))
             if i == 0:
@@ -350,11 +362,6 @@ def tile_graphlearner_ib_pa_t_kernel(
         for half in range(2):
             loads.append((half, 3, load_w_out, (half,)))
         loads = sorted(loads, key=lambda l: l[0:2])
-        load_w_user(0)
-        load_w_user(1)
-        nc.gpsimd.dma_start(out=brow[0:2, 0:512], in_=b_user.rearrange("(g f) -> g f", g=2))
-        nc.gpsimd.dma_start(out=brow[0:1, 512:768], in_=bl_img.rearrange("(a o) -> a o", a=1))
-        nc.gpsimd.dma_start(out=brow[1:2, 512:768], in_=bl_txt.rearrange("(a o) -> a o", a=1))
 
         def load_until(limit):
             for item in [l for l in loads if l[0] <= limit]:
@@ -362,45 +369,50 @@ def tile_graphlearner_ib_pa_t_kernel(
                 need, kind, call, args = item
                 call(*args)
 
-        load_until(2 - 1)
+        load_w_user(0)
+        load_until(-LEAD - 2)
+        load_w_user(1)
+        nc.gpsimd.dma_start(out=brow[0:2, 0:512], in_=b_user.rearrange("(g f) -> g f", g=2))
+        nc.gpsimd.dma_start(out=brow[0:1, 512:768], in_=bl_img.rearrange("(a o) -> a o", a=1))
+        nc.gpsimd.dma_start(out=brow[1:2, 512:768], in_=bl_txt.rearrange("(a o) -> a o", a=1))
+
+        load_until(-LEAD + 3)
         transpose_w_user(0)
-        transpose_w_user(1)
-        quantise_w_user(0)
         transpose_feat(ORDER[0])
+        quantise_w_user(0)
+        quantise_feat(ORDER[0])
+        transpose_w_user(1)
         quantise_w_user(1)
         bank = psum.tile([P, 4, P], BF16, name="bank_bf", tag="bank")
         for t in range(4):
             nc.tensor.transpose(out=bank[:, t, :], in_=brow[:, t:512:4], identity=ident_bf[:])
         nc.vector.tensor_copy(out=bu[:], in_=bank[:, :, 0:PASSES].rearrange("p t g -> p g t"))
-        quantise_feat(ORDER[0])
         for half in range(PASSES):
             nc.vector.tensor_copy(out=bu_wide[:, half], in_=bu[:, half : half + 1, :].to_broadcast([P, P, 4]))
 
-        for s in range(-LEAD, HALVES + 3):
+        for s in range(-LEAD, HALVES + 2):
             load_until(s + 2)
-            if half_at(s - 4) is not None:
-                store(*half_at(s - 4))
-            if s - 1 in sum_at:
-                scale_sum(*sum_at[s - 1])
-            todo = []
+            todo = [(sum_block, (0, x, g)) for x in EARLY.get(s, ()) for g in range(PASSES)]
             if half_at(s) is not None:
                 r, i = half_at(s)
                 for x in range(2):
                     if r in PE_BLOCKS:
                         for b in PE_BLOCKS[r][i]:
-                            for g in range(PASSES):
+                            for g in range(PASSES if b > 0 else 0):
                                 todo.append((sum_block, (b, x, g)))
                     else:
                         todo.append((transpose_sum, (2 * r + i, x)))
-            if half_at(s - 3) is not None:
+            if half_at(s - 3) is not None and s - 3 < HALVES - 2:
                 stage2(*half_at(s - 3))
-            for half in range(PASSES):
-                if half_at(s + LEAD) is not None:
-                    r, i = half_at(s + LEAD)
-                    stage1(r, i, half)
+            if half_at(s + LEAD) is not None:
+                r, i = half_at(s + LEAD)
+                stage1(r, i, 0)
+                if s == -LEAD:
+                    transpose_feat(half_at(2)[0])
+                stage1(r, i, 1)
             for call, args in todo:
                 call(*args)
-            if (s + LEAD) % 2 == 0 and half_at(s + LEAD + 2) is not None:
+            if s > -LEAD and (s + LEAD) % 2 == 0 and half_at(s + LEAD + 2) is not None:
                 transpose_feat(half_at(s + LEAD + 2)[0])
             if s in (0, 1):
                 transpose_w_out(s)
@@ -410,18 +422,29 @@ def tile_graphlearner_ib_pa_t_kernel(
                 bank = psum.tile([P, O], F32, name="bank_bl", tag="bank")
                 nc.tensor.matmul(out=bank[:], lhsT=ones[:], rhs=brow[:, 512:768], start=True, stop=True)
                 nc.scalar.copy(out=bl[:], in_=bank[:])
-            if s % 2 == 0 and half_at(s - 2) is not None:
+            if s % 2 == 0 and half_at(s - 2) is not None and s < HALVES:
                 quantise_means(half_at(s - 2)[0])
+            if HALVES - 1 <= s <= HALVES:
+                quantise_half(*half_at(s - 1))
+            if s >= HALVES:
+                stage2(*half_at(s - 2))
             if half_at(s + LEAD - 1) is not None:
                 quantise_u(*half_at(s + LEAD - 1))
             if (s + LEAD) % 2 == 1 and half_at(s + LEAD + 1) is not None:
                 quantise_feat(half_at(s + LEAD + 1)[0])
-            if half_at(s - 3) is not None:
-                add_bias(*half_at(s - 3))
+            for k in (s - 3, s - 2):
+                if half_at(k) is not None and (k < HALVES - 2) == (k == s - 3):
+                    add_bias(*half_at(k))
             if half_at(s + LEAD) is not None:
                 copy_u(*half_at(s + LEAD))
             if s in sum_at:
                 vector_sum(*sum_at[s])
-            if half_at(s - 3) is not None:
-                relu(*half_at(s - 3))
-        store(*half_at(HALVES - 1))
+            if s - 1 in sum_at:
+                scale_sum(*sum_at[s - 1])
+            if half_at(s - 4) is not None and s - 4 < HALVES - 2:
+                store(*half_at(s - 4))
+            for k in (s - 3, s - 2):
+                if half_at(k) is not None and (k < HALVES - 2) == (k == s - 3):
+                    relu(*half_at(k))
+                    if k >= HALVES - 2:
+                        store(*half_at(k))

@@ -19,7 +19,7 @@ ORDER = (0, 1, 6, 2, 3, 7, 4, 5)
 VECTOR_ROUNDS = (6, 7,)
 GROUP = P // NODES
 BLOCK = 3 * GROUP
-PE_USERS = ROUND * (len(ORDER) - len(VECTOR_ROUNDS))
+PE_USERS = (1536, 1408)
 PE_BLOCKS = {0: ((0, 1), (2,)), 1: ((3,), (4,)), 2: ((5,), (6,)), 3: ((7,), (8,)), 4: ((9,), (10,)), 5: ((11,), (12,))}
 LEAD = 4
 EARLY = {-3: (0,), -1: (1,)}
@@ -100,7 +100,7 @@ def tile_graphlearner_ib_pa_t_kernel(
 
         def load_rows(b):
             for x in range(2):
-                for q in range(3 * b, min(3 * b + 3, -(-PE_USERS // GROUP))):
+                for q in range(3 * b, min(3 * b + 3, -(-PE_USERS[x] // GROUP))):
                     t = rows_pool.tile([P, H], BF16, name="rows", tag="rows")
                     nc.sync.dma_start(out=t[:], in_=rows_v[x][3 * GROUP * q : 3 * GROUP * q + P, :])
                     rows[(x, q)] = t
@@ -213,7 +213,7 @@ def tile_graphlearner_ib_pa_t_kernel(
 
         def sum_block(b, x, g):
             first = BLOCK * b
-            count = min(BLOCK, PE_USERS - first)
+            count = min(BLOCK, PE_USERS[x] - first)
             bank = new_bank()
             todo = [(j, t) for j in range(-(-count // GROUP)) for t in range(4)]
             for j, t in todo:
@@ -237,7 +237,7 @@ def tile_graphlearner_ib_pa_t_kernel(
             nc.vector.tensor_tensor(out=total[:], in0=part[:], in1=by_h[2], op=ALU.add)
 
         def scale_sum(s, x):
-            t = deep.tile([P, H], BF16, name="mean", tag="mean")
+            t = deep.tile([P, H], BF16, name="mean", tag="mean", bufs=6)
             vmean[(s, x)] = t
             nc.scalar.activation(out=t[:], in_=vsum[(s, x)][:].rearrange("p h m e -> p (h m e)"), func=ACT.Copy, scale=1.0 / NODES)
 
@@ -315,12 +315,8 @@ def tile_graphlearner_ib_pa_t_kernel(
             m_codes, m_scales = m_q[r]
             u_codes, u_scales = u_q[(r, i)]
             cols = slice(P * i, P * (i + 1))
-            left = []
-            for g in range(PASSES):
-                left.append((u_codes[:, g, :], u_scales[:, g, :], 1, g))
-                left.append((u_codes[:, g, :], u_scales[:, g, :], 3, g))
-                left.append((m_codes[:, 0, g, cols], m_scales[:, 0, g, cols], 0, g))
-                left.append((m_codes[:, 1, g, cols], m_scales[:, 1, g, cols], 2, g))
+            left = [(u_codes[:, g, :], u_scales[:, g, :], m, g) for m in (1, 3) for g in range(PASSES)]
+            left += [(m_codes[:, x, g, cols], m_scales[:, x, g, cols], 2 * x, g) for x in range(2) for g in range(PASSES)]
             for n, (codes, scales, m, g) in enumerate(left):
                 nc.tensor.matmul_mx(
                     out=bank[:],
@@ -333,7 +329,7 @@ def tile_graphlearner_ib_pa_t_kernel(
                 )
 
         def add_bias(r, i):
-            t = deep.tile([P, O], F32, name="res", tag="res")
+            t = deep.tile([P, O], F32, name="res", tag="res", bufs=8)
             res[(r, i)] = t
             nc.vector.tensor_tensor(out=t[:], in0=o_bank[(r, i)][:], in1=bl[:], op=ALU.add)
 
@@ -348,7 +344,7 @@ def tile_graphlearner_ib_pa_t_kernel(
         def half_at(s):
             return (ORDER[s // 2], s % 2) if 0 <= s < HALVES else None
 
-        sum_at = {0: (12, 0), 1: (12, 1), 2: (13, 0), 3: (13, 1), 6: (14, 0), 7: (14, 1), 8: (15, 0), 9: (15, 1)}
+        sum_at = {0: (12, 0), 1: (12, 1), 2: (13, 0), 3: (13, 1), 6: (14, 0), 7: (14, 1), 8: (15, 0), 9: (15, 1), 12: (11, 1)}
         loads = []
         for s in range(HALVES):
             r, i = half_at(s)
@@ -396,7 +392,7 @@ def tile_graphlearner_ib_pa_t_kernel(
             if half_at(s) is not None:
                 r, i = half_at(s)
                 for x in range(2):
-                    if r in PE_BLOCKS:
+                    if P * (2 * r + i) < PE_USERS[x]:
                         for b in PE_BLOCKS[r][i]:
                             for g in range(PASSES if b > 0 else 0):
                                 todo.append((sum_block, (b, x, g)))

from contextlib import ExitStack

import concourse.mybir as mybir
from concourse.masks import make_identity

F32 = mybir.dt.float32
BF16 = mybir.dt.bfloat16
U32 = mybir.dt.uint32
U8 = mybir.dt.uint8
FP8X4 = mybir.dt.float8_e4m3fn_x4
ACT = mybir.ActivationFunctionType
ALU = mybir.AluOpType

P = 128
USERS, NODES, H, O = 2048, 3, 1024, 256
ROUND = 2 * P
PASSES = H // (4 * P)
ORDER = (0, 1, 6, 2, 3, 7, 4, 5)
VECTOR_ROUNDS = (6, 7,)
GROUP = P // NODES
BLOCK = 3 * GROUP
PE_USERS = (1536, 1408)
PE_BLOCKS = {0: ((0, 1), (2,)), 1: ((3,), (4,)), 2: ((5,), (6,)), 3: ((7,), (8,)), 4: ((9,), (10,)), 5: ((11,), (12,))}
LEAD = 4
EARLY = {-3: (0,), -1: (1,)}
FLOPS = 2 * USERS * H * H + 4 * 2 * USERS * H * O


def tile_graphlearner_ib_pa_t_kernel(
    tc,
    input_text,
    input_img,
    input_compress,
    base_text_features,
    base_img_features,
    W_user,
    b_user,
    Wl_img,
    bl_img,
    Wr_img,
    Wl_txt,
    bl_txt,
    Wr_txt,
    out,
):
    nc = tc.nc
    text_v = input_text.rearrange("(r p i) o d -> r p i (o d)", p=P, i=2)
    imgf_v = input_img.rearrange("(r p i) o d -> r p i (o d)", p=P, i=2)
    comp_v = input_compress.rearrange("(r p i) d -> r p i d", p=P, i=2)
    bases = (base_img_features, base_text_features)
    rows_v = tuple(b.rearrange("b n h -> (b n) h") for b in bases)
    users_v = tuple(b.rearrange("(s p) n h -> s p n h", p=P) for b in bases)
    out_v = out.rearrange("(s p) o -> s p o", p=P)
    wu_v = W_user.rearrange("(g p t) f -> g p t f", p=P, t=4)

    with ExitStack() as stack:
        keep = stack.enter_context(tc.tile_pool(name="keep", bufs=1))
        rows_pool = stack.enter_context(tc.tile_pool(name="rows", bufs=18))
        work = stack.enter_context(tc.tile_pool(name="work", bufs=2))
        deep = stack.enter_context(tc.tile_pool(name="deep", bufs=4))
        psum = stack.enter_context(tc.psum_pool(name="psum", bufs=8))
        stack.enter_context(tc.manual_schedule())

        ident = keep.tile([P, P], F32, name="ident")
        make_identity(nc, ident[:])
        warm = keep.tile([P, 1], F32, name="warm")
        nc.vector.memset(warm[:], 0.0)
        nc.scalar.activation(out=warm[:], in_=warm[:], func=ACT.Relu)
        brow = keep.tile([P, 768], BF16, name="brow")
        nc.gpsimd.memset(brow[:], 0.0)
        pick = keep.tile([P, GROUP], BF16, name="pick")
        nc.gpsimd.memset(pick[:], 1.0)
        nc.gpsimd.affine_select(
            out=pick[:], in_=pick[:], pattern=[[-NODES, GROUP]], compare_op=ALU.is_ge, fill=0.0, base=0, channel_multiplier=1
        )
        nc.gpsimd.affine_select(
            out=pick[:], in_=pick[:], pattern=[[NODES, GROUP]], compare_op=ALU.is_ge, fill=0.0, base=NODES - 1, channel_multiplier=-1
        )
        ident_bf = keep.tile([P, P], BF16, name="ident_bf")
        make_identity(nc, ident_bf[:])
        ones = keep.tile([P, P], BF16, name="ones")
        nc.gpsimd.memset(ones[:], 1.0)
        bu = keep.tile([P, PASSES, 4], F32, name="bu")
        bu_wide = keep.tile([P, PASSES, P, 4], F32, name="bu_wide")
        bl = keep.tile([P, O], F32, name="bl")

        wu_codes = keep.tile([P, 8, PASSES, P], U32, name="wu_codes", align_bytes=64)
        wu_scales = keep.tile([P, 8, PASSES, P], U8, name="wu_scales", align_bytes=64)
        ws_codes = keep.tile([P, 4, PASSES, O], U32, name="ws_codes", align_bytes=64)
        ws_scales = keep.tile([P, 4, PASSES, O], U8, name="ws_scales", align_bytes=64)

        raw, wgroup, rows, vnodes, vsum, vmean, feats = {}, {}, {}, {}, {}, {}, {}
        mg, m_q, fg, f_q, ug, u_q, u_bank, o_bank, res = {}, {}, {}, {}, {}, {}, {}, {}, {}

        def quantise(values, codes, scales):
            nc.vector.quantize_mx(out=codes.bitcast(FP8X4), scales=scales, in_=values)

        def new_bank():
            return psum.tile([P, 4, P], F32, name="bank", tag="bank")

        def load_rows(b):
            for x in range(2):
                for q in range(3 * b, min(3 * b + 3, -(-PE_USERS[x] // GROUP))):
                    t = rows_pool.tile([P, H], BF16, name="rows", tag="rows")
                    nc.sync.dma_start(out=t[:], in_=rows_v[x][3 * GROUP * q : 3 * GROUP * q + P, :])
                    rows[(x, q)] = t

        def load_vector(s, x):
            t = work.tile([P, NODES, H], BF16, name="vnodes", tag="vnodes", bufs=3)
            nc.sync.dma_start(out=t[:], in_=users_v[x][s])
            vnodes[(s, x)] = t

        def load_feat(r):
            t = work.tile([P, 2, H], BF16, name="feat", tag="feat", bufs=3)
            nc.sync.dma_start(out=t[:, :, 0:256], in_=text_v[r])
            nc.sync.dma_start(out=t[:, :, 256:512], in_=imgf_v[r])
            nc.sync.dma_start(out=t[:, :, 512:1024], in_=comp_v[r])
            feats[r] = t

        def load_w_user(half):
            t = work.tile([P, 4, H], BF16, name="w_raw", tag="w_raw")
            for i in range(4):
                nc.sync.dma_start(out=t[:, i : i + 1, :], in_=wu_v[half][:, i : i + 1, :])
            raw[("u", half)] = t

        def load_w_out(half):
            t = work.tile([P, 4, H], BF16, name="w_raw", tag="w_raw")
            for i, w in enumerate(((Wl_img, Wr_img), (Wl_txt, Wr_txt))[half]):
                nc.sync.dma_start(out=t[:, 2 * i : 2 * i + 2, :], in_=w.rearrange("(p a) h -> p a h", a=2))
            raw[("o", half)] = t

        def transpose_words(bank, slot, words, g, h):
            nc.tensor.transpose(out=bank[:, slot, :], in_=words[:, 256 * g + h : 256 * (g + 1) : 2], identity=ident[:])

        def transpose_w_user(half):
            wg = work.tile([P, 4, PASSES, 4 * P], BF16, name="wg", tag="wgroup", align_bytes=64)
            wgroup[("u", half)] = wg
            for t in range(4):
                words = raw[("u", half)][:, t, :].bitcast(F32)
                bank = new_bank()
                for g in range(PASSES):
                    for h in range(2):
                        transpose_words(bank, 2 * g + h, words, g, h)
                copy = nc.scalar.copy if t % 2 == 0 else nc.vector.tensor_copy
                copy(
                    out=wg[:, t, :, :].bitcast(F32).rearrange("p g (r u) -> p g r u", u=2),
                    in_=bank[:].rearrange("p (g u) r -> p g r u", u=2),
                )

        def quantise_w_user(half):
            cs = slice(4 * half, 4 * half + 4)
            quantise(
                wgroup[("u", half)][:].rearrange("p j g w -> p (j g w)"),
                wu_codes[:, cs].rearrange("p j g r -> p (j g r)"),
                wu_scales[:, cs].rearrange("p j g r -> p (j g r)"),
            )

        def transpose_pairs(src, dst):
            for g in range(PASSES):
                bank = new_bank()
                for i in range(2):
                    for h in range(2):
                        transpose_words(bank, 2 * i + h, src[:, i, :].bitcast(F32), g, h)
                nc.scalar.copy(out=dst[:, g, :].bitcast(F32).rearrange("p (r k) -> p r k", k=4), in_=bank[:].rearrange("p k r -> p r k"))

        def transpose_w_out(half):
            wg = work.tile([P, 2, PASSES, 4 * O], BF16, name="wg", tag="wgroup", align_bytes=64)
            wgroup[("o", half)] = wg
            for i in range(2):
                transpose_pairs(raw[("o", half)][:, 2 * i : 2 * i + 2, :], wg[:, i, :, :])

        def quantise_w_out(half):
            ms = slice(2 * half, 2 * half + 2)
            quantise(
                wgroup[("o", half)][:].rearrange("p m g w -> p (m g w)"),
                ws_codes[:, ms].rearrange("p m g o -> p (m g o)"),
                ws_scales[:, ms].rearrange("p m g o -> p (m g o)"),
            )

        def transpose_feat(r):
            t = work.tile([P, PASSES, 4 * ROUND], BF16, name="fg", tag="fg", align_bytes=64)
            fg[r] = t
            transpose_pairs(feats[r], t)

        def quantise_feat(r):
            codes = work.tile([P, PASSES, ROUND], U32, name="f_codes", tag="f_codes", align_bytes=64)
            scales = work.tile([P, PASSES, ROUND], U8, name="f_scales", tag="f_scales", align_bytes=64)
            f_q[r] = (codes, scales)
            quantise(
                fg[r][:].rearrange("p g w -> p (g w)"),
                codes[:].rearrange("p g n -> p (g n)"),
                scales[:].rearrange("p g n -> p (g n)"),
            )

        def mean_tile(r):
            if r not in mg:
                t = deep.tile([P, 2, PASSES, ROUND, 4], BF16, name="mg", tag="mg", align_bytes=64, bufs=3)
                mg[r] = t
            return mg[r]

        def mean_copy(x, g, first, count, bank):
            lo = first
            while lo < first + count:
                r = lo // ROUND
                hi = min(first + count, ROUND * (r + 1))
                nc.scalar.activation(
                    out=mean_tile(r)[:, x, g, lo - ROUND * r : hi - ROUND * r, :],
                    in_=bank[:, :, lo - first : hi - first].rearrange("p t n -> p n t"),
                    func=ACT.Copy,
                    scale=1.0 / NODES,
                )
                lo = hi

        def sum_block(b, x, g):
            first = BLOCK * b
            count = min(BLOCK, PE_USERS[x] - first)
            bank = new_bank()
            todo = [(j, t) for j in range(-(-count // GROUP)) for t in range(4)]
            for j, t in todo:
                n = min(GROUP, count - GROUP * j)
                nc.tensor.matmul(
                    out=bank[:, t, GROUP * j : GROUP * j + n],
                    lhsT=rows[(x, 3 * b + j)][:, 512 * g + t : 512 * (g + 1) : 4],
                    rhs=pick[:, 0:n],
                    start=(j, t) == todo[0],
                    stop=(j, t) == todo[-1],
                )
            mean_copy(x, g, first, count, bank)

        def vector_sum(s, x):
            n = vnodes[(s, x)]
            part = work.tile([P, 2, H // 4, 2], F32, name="part", tag="part")
            total = work.tile([P, 2, H // 4, 2], F32, name="total", tag="total", bufs=3)
            vsum[(s, x)] = total
            by_h = [n[:, i, :].rearrange("p (m h e) -> p h m e", h=2, e=2) for i in range(NODES)]
            nc.vector.tensor_tensor(out=part[:], in0=by_h[0], in1=by_h[1], op=ALU.add)
            nc.vector.tensor_tensor(out=total[:], in0=part[:], in1=by_h[2], op=ALU.add)

        def scale_sum(s, x):
            t = deep.tile([P, H], BF16, name="mean", tag="mean", bufs=6)
            vmean[(s, x)] = t
            nc.scalar.activation(out=t[:], in_=vsum[(s, x)][:].rearrange("p h m e -> p (h m e)"), func=ACT.Copy, scale=1.0 / NODES)

        def transpose_sum(s, x):
            words = vmean[(s, x)][:].bitcast(F32)
            bank = new_bank()
            for g in range(PASSES):
                for h in range(2):
                    nc.tensor.transpose(out=bank[:, 2 * g + h, :], in_=words[:, 256 * h + P * g : 256 * h + P * (g + 1)], identity=ident[:])
            r, i = divmod(s, 2)
            nc.scalar.copy(
                out=mean_tile(r)[:, x, :, P * i : P * (i + 1), :].rearrange("p g n t -> p g (n t)").bitcast(F32).rearrange("p g (n h) -> p g n h", h=2),
                in_=bank[:].rearrange("p (g h) n -> p g n h", h=2),
            )

        def quantise_means(r):
            codes = work.tile([P, 2, PASSES, ROUND], U32, name="m_codes", tag="m_codes", align_bytes=64)
            scales = work.tile([P, 2, PASSES, ROUND], U8, name="m_scales", tag="m_scales", align_bytes=64)
            m_q[r] = (codes, scales)
            quantise(
                mg[r][:].rearrange("p x g n t -> p (x g n t)"),
                codes[:].rearrange("p x g n -> p (x g n)"),
                scales[:].rearrange("p x g n -> p (x g n)"),
            )

        def quantise_half(r, i):
            if i == 0:
                codes = work.tile([P, 2, PASSES, ROUND], U32, name="m_codes", tag="m_codes", align_bytes=64)
                scales = work.tile([P, 2, PASSES, ROUND], U8, name="m_scales", tag="m_scales", align_bytes=64)
                m_q[r] = (codes, scales)
            codes, scales = m_q[r]
            cols = slice(P * i, P * (i + 1))
            for x in range(2):
                for g in range(PASSES):
                    quantise(mg[r][:, x, g, cols].rearrange("p n t -> p (n t)"), codes[:, x, g, cols], scales[:, x, g, cols])

        def stage1(r, i, half):
            codes, scales = f_q[r]
            cols = slice(P * i, P * (i + 1))
            bank = new_bank()
            u_bank[(r, i, half)] = bank
            for t in range(4):
                for g in range(PASSES):
                    nc.tensor.matmul_mx(
                        out=bank[:, t, :],
                        lhsT=wu_codes[:, 4 * half + t, g, :].bitcast(FP8X4),
                        lhsT_scale=wu_scales[:, 4 * half + t, g, :],
                        rhs=codes[:, g, cols].bitcast(FP8X4),
                        rhs_scale=scales[:, g, cols],
                        start=(g == 0),
                        stop=(g == PASSES - 1),
                    )

        def copy_u(r, i):
            ut = work.tile([P, PASSES, P, 4], BF16, name="ug", tag="ug", align_bytes=64)
            ug[(r, i)] = ut
            for half in range(PASSES):
                nc.vector.tensor_tensor(
                    out=ut[:, half], in0=u_bank[(r, i, half)][:].rearrange("p t n -> p n t"), in1=bu_wide[:, half], op=ALU.add
                )

        def quantise_u(r, i):
            codes = deep.tile([P, PASSES, P], U32, name="u_codes", tag="u_codes", align_bytes=64, bufs=8)
            scales = deep.tile([P, PASSES, P], U8, name="u_scales", tag="u_scales", align_bytes=64, bufs=8)
            u_q[(r, i)] = (codes, scales)
            quantise(
                ug[(r, i)][:].rearrange("p g n t -> p (g n t)"),
                codes[:].rearrange("p g n -> p (g n)"),
                scales[:].rearrange("p g n -> p (g n)"),
            )

        def stage2(r, i):
            bank = psum.tile([P, O], F32, name="ob", tag="bank")
            o_bank[(r, i)] = bank
            m_codes, m_scales = m_q[r]
            u_codes, u_scales = u_q[(r, i)]
            cols = slice(P * i, P * (i + 1))
            left = [(u_codes[:, g, :], u_scales[:, g, :], m, g) for m in (1, 3) for g in range(PASSES)]
            left += [(m_codes[:, x, g, cols], m_scales[:, x, g, cols], 2 * x, g) for x in range(2) for g in range(PASSES)]
            for n, (codes, scales, m, g) in enumerate(left):
                nc.tensor.matmul_mx(
                    out=bank[:],
                    lhsT=codes.bitcast(FP8X4),
                    lhsT_scale=scales,
                    rhs=ws_codes[:, m, g, :].bitcast(FP8X4),
                    rhs_scale=ws_scales[:, m, g, :],
                    start=(n == 0),
                    stop=(n == len(left) - 1),
                )

        def add_bias(r, i):
            t = deep.tile([P, O], F32, name="res", tag="res", bufs=8)
            res[(r, i)] = t
            nc.vector.tensor_tensor(out=t[:], in0=o_bank[(r, i)][:], in1=bl[:], op=ALU.add)

        def relu(r, i):
            nc.scalar.activation(out=res[(r, i)][:], in_=res[(r, i)][:], func=ACT.Relu)

        def store(r, i):
            nc.scalar.dma_start(out=out_v[2 * r + i], in_=res[(r, i)][:])

        HALVES = 2 * len(ORDER)

        def half_at(s):
            return (ORDER[s // 2], s % 2) if 0 <= s < HALVES else None

        sum_at = {0: (12, 0), 1: (12, 1), 2: (13, 0), 3: (13, 1), 6: (14, 0), 7: (14, 1), 8: (15, 0), 9: (15, 1), 12: (11, 1)}
        loads = []
        for s in range(HALVES):
            r, i = half_at(s)
            if r in PE_BLOCKS:
                for b in PE_BLOCKS[r][i]:
                    loads.append((s if b > 0 else min(EARLY), 1, load_rows, (b,)))
            if s in sum_at:
                loads.append((s, 2, load_vector, sum_at[s]))
            if i == 0:
                loads.append((s - LEAD - 2, 0, load_feat, (r,)))
        for half in range(2):
            loads.append((half, 3, load_w_out, (half,)))
        loads = sorted(loads, key=lambda l: l[0:2])

        def load_until(limit):
            for item in [l for l in loads if l[0] <= limit]:
                loads.remove(item)
                need, kind, call, args = item
                call(*args)

        load_w_user(0)
        load_until(-LEAD - 2)
        load_w_user(1)
        nc.gpsimd.dma_start(out=brow[0:2, 0:512], in_=b_user.rearrange("(g f) -> g f", g=2))
        nc.gpsimd.dma_start(out=brow[0:1, 512:768], in_=bl_img.rearrange("(a o) -> a o", a=1))
        nc.gpsimd.dma_start(out=brow[1:2, 512:768], in_=bl_txt.rearrange("(a o) -> a o", a=1))

        load_until(-LEAD + 3)
        transpose_w_user(0)
        transpose_feat(ORDER[0])
        quantise_w_user(0)
        quantise_feat(ORDER[0])
        transpose_w_user(1)
        quantise_w_user(1)
        bank = psum.tile([P, 4, P], BF16, name="bank_bf", tag="bank")
        for t in range(4):
            nc.tensor.transpose(out=bank[:, t, :], in_=brow[:, t:512:4], identity=ident_bf[:])
        nc.vector.tensor_copy(out=bu[:], in_=bank[:, :, 0:PASSES].rearrange("p t g -> p g t"))
        for half in range(PASSES):
            nc.vector.tensor_copy(out=bu_wide[:, half], in_=bu[:, half : half + 1, :].to_broadcast([P, P, 4]))

        for s in range(-LEAD, HALVES + 2):
            load_until(s + 2)
            todo = [(sum_block, (0, x, g)) for x in EARLY.get(s, ()) for g in range(PASSES)]
            if half_at(s) is not None:
                r, i = half_at(s)
                for x in range(2):
                    if P * (2 * r + i) < PE_USERS[x]:
                        for b in PE_BLOCKS[r][i]:
                            for g in range(PASSES if b > 0 else 0):
                                todo.append((sum_block, (b, x, g)))
                    else:
                        todo.append((transpose_sum, (2 * r + i, x)))
            if half_at(s - 3) is not None and s - 3 < HALVES - 2:
                stage2(*half_at(s - 3))
            if half_at(s + LEAD) is not None:
                r, i = half_at(s + LEAD)
                stage1(r, i, 0)
                if s == -LEAD:
                    transpose_feat(half_at(2)[0])
                stage1(r, i, 1)
            for call, args in todo:
                call(*args)
            if s > -LEAD and (s + LEAD) % 2 == 0 and half_at(s + LEAD + 2) is not None:
                transpose_feat(half_at(s + LEAD + 2)[0])
            if s in (0, 1):
                transpose_w_out(s)
            if s in (1, 2):
                quantise_w_out(s - 1)
            if s == 0:
                bank = psum.tile([P, O], F32, name="bank_bl", tag="bank")
                nc.tensor.matmul(out=bank[:], lhsT=ones[:], rhs=brow[:, 512:768], start=True, stop=True)
                nc.scalar.copy(out=bl[:], in_=bank[:])
            if s % 2 == 0 and half_at(s - 2) is not None and s < HALVES:
                quantise_means(half_at(s - 2)[0])
            if HALVES - 1 <= s <= HALVES:
                quantise_half(*half_at(s - 1))
            if s >= HALVES:
                stage2(*half_at(s - 2))
            if half_at(s + LEAD - 1) is not None:
                quantise_u(*half_at(s + LEAD - 1))
            if (s + LEAD) % 2 == 1 and half_at(s + LEAD + 1) is not None:
                quantise_feat(half_at(s + LEAD + 1)[0])
            for k in (s - 3, s - 2):
                if half_at(k) is not None and (k < HALVES - 2) == (k == s - 3):
                    add_bias(*half_at(k))
            if half_at(s + LEAD) is not None:
                copy_u(*half_at(s + LEAD))
            if s in sum_at:
                vector_sum(*sum_at[s])
            if s - 1 in sum_at:
                scale_sum(*sum_at[s - 1])
            if half_at(s - 4) is not None and s - 4 < HALVES - 2:
                store(*half_at(s - 4))
            for k in (s - 3, s - 2):
                if half_at(k) is not None and (k < HALVES - 2) == (k == s - 3):
                    relu(*half_at(k))
                    if k >= HALVES - 2:
                        store(*half_at(k))
